import numpy as np
import ml_dtypes


def mxq(x, axis, fmt="e4m3"):
    dtype, down = {"e4m3": (ml_dtypes.float8_e4m3fn, 7), "e5m2": (ml_dtypes.float8_e5m2, 14)}[fmt]
    v = np.moveaxis(np.asarray(x, np.float32).astype(ml_dtypes.bfloat16).astype(np.float64), axis, -1)
    blocks = v.reshape(v.shape[:-1] + (-1, 32))
    amax = np.abs(blocks).max(-1, keepdims=True)
    byte = np.maximum(np.where(amax > 0, np.frexp(amax)[1] - 1 + 127, 0) - down, 1)
    scale = np.exp2(byte - 127.0)
    codes = (blocks / scale).astype(np.float32).astype(dtype).astype(np.float64)
    return np.moveaxis((codes * scale).reshape(v.shape), -1, axis)


WIDE = False


def mx_kscale(k):
    if not WIDE:
        return np.ones(k)
    levels = np.array([10, -10, 5, -5, 0])
    if k % 512:
        return np.exp2(np.random.permutation(np.resize(levels, k // 32))).repeat(32)
    a = np.empty((k // 512, 16))
    for p in range(k // 512):
        a[p, :8] = np.random.permutation(np.resize(levels, 8))
        for g in range(8):
            far = levels[np.abs(levels - a[p, g]) >= 10]
            a[p, g + 8] = far[np.random.randint(len(far))]
    return np.exp2(a.ravel()).repeat(32)


BF16 = ml_dtypes.bfloat16


def bf(x):
    return np.asarray(x, np.float32).astype(BF16)


def f64(x):
    return np.asarray(x).astype(np.float64)


B, N_IN, N_OUT, D_IN, D_OUT = 128, 64, 16, 512, 16


def setup_inputs():
    s = mx_kscale(D_IN)
    inputs = np.random.standard_normal((B, N_IN, D_IN, 1)) * s[:, None]
    transform_mat = np.random.uniform(-1.0, 1.0, (1, N_IN, N_OUT, D_IN, D_OUT, 1)) * np.sqrt(3.0 / D_IN) / s[:, None, None]
    return {"inputs": bf(inputs), "transform_mat": bf(transform_mat)}


def reference(inputs, transform_mat):
    xq = mxq(f64(inputs)[..., 0], 2, "e4m3")
    wq = mxq(f64(transform_mat)[0, ..., 0], 2, "e4m3")
    prod = xq.transpose(1, 0, 2) @ wq.transpose(0, 2, 1, 3).reshape(N_IN, D_IN, N_OUT * D_OUT)
    votes = prod.reshape(N_IN, B, N_OUT, D_OUT).transpose(1, 0, 2, 3)
    return votes[..., None]

@@ -1,0 +1,238 @@
+from contextlib import ExitStack
+
+import concourse.mybir as mybir
+from concourse.masks import make_identity
+
+F32 = mybir.dt.float32
+BF16 = mybir.dt.bfloat16
+U32 = mybir.dt.uint32
+U8 = mybir.dt.uint8
+FP8X4 = mybir.dt.float8_e4m3fn_x4
+
+P = 128
+N_IN = 64
+N_OUT = 16
+D_IN = 512
+D_OUT = 16
+COLS = N_OUT * D_OUT
+GR = 4
+N_Q = N_IN // GR
+W_BUFS = 8
+X_BUFS = 5
+
+FLOPS = 2 * P * N_IN * D_IN * COLS
+
+
+def tile_transforming_kernel(tc, inputs, transform_mat, out):
+    nc = tc.nc
+    w_view = transform_mat.rearrange("z (q n) m (g u r) o x -> q u (z n m) g (r o x)", q=N_Q, u=2, r=16)
+    x_view = inputs.rearrange("b n i x -> b (n i x)")
+    o_view = out.rearrange("b n m o x -> b (n m o x)")
+
+    with ExitStack() as stack:
+        const = stack.enter_context(tc.tile_pool(name="const", bufs=1))
+        w_pool = stack.enter_context(tc.tile_pool(name="w_pool", bufs=W_BUFS))
+        x_pool = stack.enter_context(tc.tile_pool(name="x_pool", bufs=X_BUFS))
+        p_pool = stack.enter_context(tc.tile_pool(name="p_pool", bufs=3))
+        g_pool = stack.enter_context(tc.tile_pool(name="g_pool", bufs=3))
+        xg_pool = stack.enter_context(tc.tile_pool(name="xg_pool", bufs=2))
+        wq_pool = stack.enter_context(tc.tile_pool(name="wq_pool", bufs=3))
+        xq_pool = stack.enter_context(tc.tile_pool(name="xq_pool", bufs=4))
+        o_pool = stack.enter_context(tc.tile_pool(name="o_pool", bufs=4))
+        psum_w = stack.enter_context(tc.psum_pool(name="psum_w", bufs=4))
+        psum_x = stack.enter_context(tc.psum_pool(name="psum_x", bufs=2))
+        psum_o = stack.enter_context(tc.psum_pool(name="psum_o", bufs=2))
+
+        ident = const.tile([P, P], F32)
+        make_identity(nc, ident[:])
+        ident_b = const.tile([P, P], BF16)
+        nc.vector.tensor_copy(out=ident_b[:], in_=ident[:])
+
+        w_raw = {}
+        x_raw = {}
+        x_pair = {}
+        w_bank = {}
+        x_bank = {}
+        w_grp = {}
+        w_codes = {}
+        w_scales = {}
+        x_codes = {}
+        x_scales = {}
+        x_grp = {}
+        acc = {}
+        o_sb = {}
+
+        def load_w(q):
+            w_raw[q] = w_pool.tile([P, D_IN * D_OUT // 2], BF16, name="w_raw")
+            for u in range(2):
+                nc.sync.dma_start(
+                    out=w_raw[q][u:P:2, :].rearrange("p (g c) -> p g c", g=16), in_=w_view[q, u]
+                )
+
+        def load_x(q0, nq):
+            t = x_pool.tile([P, 2 * GR * D_IN], BF16, name="x_raw")
+            width = nq * GR * D_IN
+            nc.sync.dma_start(out=t[:, 0:width], in_=x_view[:, q0 * GR * D_IN : q0 * GR * D_IN + width])
+            for k in range(nq):
+                x_raw[q0 + k] = t[:, k * GR * D_IN : (k + 1) * GR * D_IN]
+
+        def x_pairs(q):
+            x_pair[q] = p_pool.tile([P, GR * D_IN], BF16, name="x_pair")
+            nc.vector.tensor_copy(
+                out=x_pair[q][:].rearrange("b (e h j u) -> b e h j u", e=2, j=8, u=2),
+                in_=x_raw[q].rearrange("b (h u j e) -> b e h j u", u=2, j=8, e=2),
+            )
+
+        def w_transposes(q):
+            rows = w_raw[q][:].rearrange("r (a e o) -> r e o a", e=2, o=D_OUT)
+            for g in range(4):
+                wt = psum_w.tile([P, 1024], BF16, name="wt")
+                w_bank[(q, g)] = wt
+                dst = wt[:].rearrange("p (n o m e u) -> p o e n m u", n=GR, o=4, e=2, u=2)
+                for o in range(4):
+                    for e in range(2):
+                        nc.tensor.transpose(dst[:, o, e], rows[:, e, 4 * g + o, :], ident_b[:])
+
+        def w_copy(q, g, engine):
+            if q not in w_grp:
+                w_grp[q] = g_pool.tile([P, GR * COLS * 4], BF16, name="w_grp", align_bytes=64)
+            dst = w_grp[q][:].bitcast(F32).rearrange("p (n g c) -> p n g c", n=GR, g=4)[:, :, g, :]
+            src = w_bank[(q, g)][:].bitcast(F32).rearrange("p (n c) -> p n c", n=GR)
+            if engine == "v":
+                nc.vector.tensor_copy(out=dst, in_=src)
+            else:
+                nc.scalar.copy(out=dst, in_=src)
+
+        def x_transposes(q):
+            words = x_pair[q][:].bitcast(F32).rearrange("b (e n a) -> b e n a", e=2, n=GR)
+            for h in range(2):
+                xt = psum_x.tile([P, 2, 2, P], F32, name="xt")
+                x_bank[(q, h)] = xt
+                for n in range(2):
+                    for e in range(2):
+                        nc.tensor.transpose(xt[:, n, e, :], words[:, e, 2 * h + n, :], ident[:])
+
+        def x_copy(q, h, engine):
+            if q not in x_grp:
+                x_grp[q] = xg_pool.tile([P, GR * D_IN], BF16, name="x_grp", align_bytes=64)
+            dst = x_grp[q][:].bitcast(F32).rearrange("p (h n b e) -> p h n b e", h=2, n=2, e=2)[:, h]
+            src = x_bank[(q, h)][:].rearrange("p n e b -> p n b e")
+            if engine == "v":
+                nc.vector.tensor_copy(out=dst, in_=src)
+            else:
+                nc.scalar.copy(out=dst, in_=src)
+
+        def x_quant(q):
+            x_codes[q] = xq_pool.tile([P, GR * P], U32, name="x_codes", align_bytes=64)
+            x_scales[q] = xq_pool.tile([P, GR * P], U8, name="x_scales", align_bytes=64)
+            nc.vector.quantize_mx(out=x_codes[q][:].bitcast(FP8X4), scales=x_scales[q][:], in_=x_grp[q][:])
+
+        def w_quant(q, parts):
+            w_codes[q] = wq_pool.tile([P, GR * COLS], U32, name="w_codes", align_bytes=64)
+            w_scales[q] = wq_pool.tile([P, GR * COLS], U8, name="w_scales", align_bytes=64)
+            width = GR * COLS // parts
+            for k in range(parts):
+                cols = slice(k * width, (k + 1) * width)
+                nc.vector.quantize_mx(
+                    out=w_codes[q][:, cols].bitcast(FP8X4),
+                    scales=w_scales[q][:, cols],
+                    in_=w_grp[q][:, 4 * k * width : 4 * (k + 1) * width],
+                )
+
+        def multiply(q, h, pool, tag):
+            bank = pool.tile([P, 2, COLS], F32, name=tag)
+            acc[(q, h)] = bank
+            for n in range(2):
+                a = 2 * h + n
+                nc.tensor.matmul_mx(
+                    out=bank[:, n, :],
+                    lhsT=x_codes[q][:, a * P : (a + 1) * P].bitcast(FP8X4),
+                    lhsT_scale=x_scales[q][:, a * P : (a + 1) * P],
+                    rhs=w_codes[q][:, a * COLS : (a + 1) * COLS].bitcast(FP8X4),
+                    rhs_scale=w_scales[q][:, a * COLS : (a + 1) * COLS],
+                    start=True,
+                    stop=True,
+                )
+
+        def evacuate(q, h, engine):
+            if q // 2 not in o_sb:
+                o_sb[q // 2] = o_pool.tile([P, 2 * GR, COLS], F32, name="o_sb")
+            n0 = GR * (q % 2) + 2 * h
+            dst = o_sb[q // 2][:, n0 : n0 + 2, :].rearrange("p n (m o) -> p n m o", m=N_OUT)
+            src = acc[(q, h)][:].rearrange("p n (o m) -> p n m o", m=N_OUT)
+            if engine == "v":
+                nc.vector.tensor_copy(out=dst, in_=src)
+            else:
+                nc.scalar.copy(out=dst, in_=src)
+
+        def store(n0, caps):
+            res = o_sb[n0 // (2 * GR)]
+            k0 = n0 % (2 * GR)
+            nc.sync.dma_start(
+                out=o_view[:, n0 * COLS : (n0 + caps) * COLS],
+                in_=res[:, k0 : k0 + caps, :].rearrange("p n c -> p (n c)"),
+            )
+
+        x_units = [(0, 1), (1, 1)] + [(q, 2) for q in range(2, N_Q, 2)]
+        first_loads = []
+        for k in range(W_BUFS):
+            first_loads.append(("w", k))
+            for j in range(X_BUFS):
+                if x_units[j][0] == k:
+                    first_loads.append(("x", j))
+
+        def refill_x(q):
+            for k in range(X_BUFS, len(x_units)):
+                freed = x_units[k - X_BUFS]
+                if freed[0] + freed[1] - 1 == q:
+                    load_x(x_units[k][0], x_units[k][1])
+
+        with tc.manual_schedule():
+            for kind, k in first_loads:
+                if kind == "w":
+                    load_w(k)
+                else:
+                    load_x(x_units[k][0], x_units[k][1])
+            w_transposes(0)
+            x_pairs(0)
+            refill_x(0)
+            load_w(W_BUFS)
+            for s in range(N_Q):
+                last = s == N_Q - 1
+                x_transposes(s)
+                x_copy(s, 0, "s")
+                x_copy(s, 1, "v")
+                if s >= 2:
+                    for h in range(2):
+                        multiply(s - 2, h, psum_o, "acc")
+                for g in range(4):
+                    w_copy(s, g, "s")
+                if s >= 2:
+                    for h in range(2):
+                        evacuate(s - 2, h, "s")
+                    if s % 2 == 1:
+                        store((s - 3) * GR, 2 * GR)
+                if s >= 1:
+                    w_quant(s - 1, 1)
+                if not last:
+                    x_pairs(s + 1)
+                    refill_x(s + 1)
+                x_quant(s)
+                if not last:
+                    w_transposes(s + 1)
+                    if s + 1 + W_BUFS < N_Q:
+                        load_w(s + 1 + W_BUFS)
+            q = N_Q - 2
+            multiply(q, 0, psum_o, "acc")
+            multiply(q, 1, psum_o, "acc")
+            w_quant(q + 1, 2)
+            evacuate(q, 0, "s")
+            evacuate(q, 1, "v")
+            store(q * GR, GR)
+            q = N_Q - 1
+            multiply(q, 0, psum_o, "acc")
+            multiply(q, 1, psum_o, "acc")
+            evacuate(q, 0, "s")
+            store(q * GR, 2)
+            evacuate(q, 1, "v")
+            store(q * GR + 2, 2)

@@ -35,7 +35,7 @@ def tile_transforming_kernel(tc, inputs, transform_mat, out):
         x_pool = stack.enter_context(tc.tile_pool(name="x_pool", bufs=X_BUFS))
         p_pool = stack.enter_context(tc.tile_pool(name="p_pool", bufs=3))
         g_pool = stack.enter_context(tc.tile_pool(name="g_pool", bufs=3))
-        xg_pool = stack.enter_context(tc.tile_pool(name="xg_pool", bufs=2))
+        xg_pool = stack.enter_context(tc.tile_pool(name="xg_pool", bufs=3))
         wq_pool = stack.enter_context(tc.tile_pool(name="wq_pool", bufs=3))
         xq_pool = stack.enter_context(tc.tile_pool(name="xq_pool", bufs=4))
         o_pool = stack.enter_context(tc.tile_pool(name="o_pool", bufs=4))
@@ -88,7 +88,7 @@ def tile_transforming_kernel(tc, inputs, transform_mat, out):
             for g in range(4):
                 wt = psum_w.tile([P, 1024], BF16, name="wt")
                 w_bank[(q, g)] = wt
-                dst = wt[:].rearrange("p (n o m e u) -> p o e n m u", n=GR, o=4, e=2, u=2)
+                dst = wt[:].rearrange("p (o e r) -> p o e r", o=4, e=2)
                 for o in range(4):
                     for e in range(2):
                         nc.tensor.transpose(dst[:, o, e], rows[:, e, 4 * g + o, :], ident_b[:])
@@ -96,8 +96,8 @@ def tile_transforming_kernel(tc, inputs, transform_mat, out):
         def w_copy(q, g, engine):
             if q not in w_grp:
                 w_grp[q] = g_pool.tile([P, GR * COLS * 4], BF16, name="w_grp", align_bytes=64)
-            dst = w_grp[q][:].bitcast(F32).rearrange("p (n g c) -> p n g c", n=GR, g=4)[:, :, g, :]
-            src = w_bank[(q, g)][:].bitcast(F32).rearrange("p (n c) -> p n c", n=GR)
+            dst = w_grp[q][:].bitcast(F32).rearrange("p (c g w) -> p c g w", g=4, w=8)[:, :, g, :]
+            src = w_bank[(q, g)][:].bitcast(F32).rearrange("p (w c) -> p c w", w=8)
             if engine == "v":
                 nc.vector.tensor_copy(out=dst, in_=src)
             else:
@@ -139,8 +139,8 @@ def tile_transforming_kernel(tc, inputs, transform_mat, out):
                     in_=w_grp[q][:, 4 * k * width : 4 * (k + 1) * width],
                 )
 
-        def multiply(q, h, pool, tag):
-            bank = pool.tile([P, 2, COLS], F32, name=tag)
+        def multiply(q, h):
+            bank = psum_o.tile([P, 2, COLS], F32, name="acc")
             acc[(q, h)] = bank
             for n in range(2):
                 a = 2 * h + n
@@ -158,8 +158,8 @@ def tile_transforming_kernel(tc, inputs, transform_mat, out):
             if q // 2 not in o_sb:
                 o_sb[q // 2] = o_pool.tile([P, 2 * GR, COLS], F32, name="o_sb")
             n0 = GR * (q % 2) + 2 * h
-            dst = o_sb[q // 2][:, n0 : n0 + 2, :].rearrange("p n (m o) -> p n m o", m=N_OUT)
-            src = acc[(q, h)][:].rearrange("p n (o m) -> p n m o", m=N_OUT)
+            dst = o_sb[q // 2][:, n0 : n0 + 2, :]
+            src = acc[(q, h)][:]
             if engine == "v":
                 nc.vector.tensor_copy(out=dst, in_=src)
             else:
@@ -193,45 +193,46 @@ def tile_transforming_kernel(tc, inputs, transform_mat, out):
                     load_w(k)
                 else:
                     load_x(x_units[k][0], x_units[k][1])
-            w_transposes(0)
             x_pairs(0)
             refill_x(0)
-            load_w(W_BUFS)
-            for s in range(N_Q):
-                last = s == N_Q - 1
-                x_transposes(s)
-                x_copy(s, 0, "s")
-                x_copy(s, 1, "v")
+            for s in range(-1, N_Q):
+                if s + 1 < N_Q:
+                    x_transposes(s + 1)
                 if s >= 2:
                     for h in range(2):
-                        multiply(s - 2, h, psum_o, "acc")
-                for g in range(4):
-                    w_copy(s, g, "s")
+                        multiply(s - 2, h)
+                if s + 2 < N_Q:
+                    x_pairs(s + 2)
+                    refill_x(s + 2)
+                if s >= 0:
+                    for g in range(4):
+                        w_copy(s, g, "s")
+                if s + 1 < N_Q:
+                    x_copy(s + 1, 0, "s")
+                    x_copy(s + 1, 1, "v")
                 if s >= 2:
-                    for h in range(2):
-                        evacuate(s - 2, h, "s")
+                    evacuate(s - 2, 0, "s")
+                    evacuate(s - 2, 1, "v" if s % 2 else "s")
                     if s % 2 == 1:
                         store((s - 3) * GR, 2 * GR)
                 if s >= 1:
                     w_quant(s - 1, 1)
-                if not last:
-                    x_pairs(s + 1)
-                    refill_x(s + 1)
-                x_quant(s)
-                if not last:
+                if s >= 0:
+                    x_quant(s)
+                if s + 1 < N_Q:
                     w_transposes(s + 1)
                     if s + 1 + W_BUFS < N_Q:
                         load_w(s + 1 + W_BUFS)
             q = N_Q - 2
-            multiply(q, 0, psum_o, "acc")
-            multiply(q, 1, psum_o, "acc")
+            multiply(q, 0)
+            multiply(q, 1)
             w_quant(q + 1, 2)
             evacuate(q, 0, "s")
-            evacuate(q, 1, "v")
+            evacuate(q, 1, "s")
             store(q * GR, GR)
             q = N_Q - 1
-            multiply(q, 0, psum_o, "acc")
-            multiply(q, 1, psum_o, "acc")
+            multiply(q, 0)
+            multiply(q, 1)
             evacuate(q, 0, "s")
             store(q * GR, 2)
             evacuate(q, 1, "v")

@@ -5,6 +5,8 @@ from concourse.masks import make_identity
 
 F32 = mybir.dt.float32
 BF16 = mybir.dt.bfloat16
+MULT = mybir.AluOpType.mult
+ADD = mybir.AluOpType.add
 U32 = mybir.dt.uint32
 U8 = mybir.dt.uint8
 FP8X4 = mybir.dt.float8_e4m3fn_x4
@@ -15,17 +17,21 @@ N_OUT = 16
 D_IN = 512
 D_OUT = 16
 COLS = N_OUT * D_OUT
-GR = 4
-N_Q = N_IN // GR
-W_BUFS = 8
-X_BUFS = 5
+CH = 8
+HC = 4
+N_CH = N_IN // CH
+N_H = N_IN // HC
+W_BUFS = 5
+X_BUFS = 4
+ROUTE = "svsvsvsv"
+EVAC = "ssss"
 
 FLOPS = 2 * P * N_IN * D_IN * COLS
 
 
 def tile_transforming_kernel(tc, inputs, transform_mat, out):
     nc = tc.nc
-    w_view = transform_mat.rearrange("z (q n) m (g u r) o x -> q u (z n m) g (r o x)", q=N_Q, u=2, r=16)
+    w_view = transform_mat.rearrange("z (s n) m i o x -> s (z n m) (i o x)", n=CH)
     x_view = inputs.rearrange("b n i x -> b (n i x)")
     o_view = out.rearrange("b n m o x -> b (n m o x)")
 
@@ -33,207 +39,210 @@ def tile_transforming_kernel(tc, inputs, transform_mat, out):
         const = stack.enter_context(tc.tile_pool(name="const", bufs=1))
         w_pool = stack.enter_context(tc.tile_pool(name="w_pool", bufs=W_BUFS))
         x_pool = stack.enter_context(tc.tile_pool(name="x_pool", bufs=X_BUFS))
-        p_pool = stack.enter_context(tc.tile_pool(name="p_pool", bufs=3))
-        g_pool = stack.enter_context(tc.tile_pool(name="g_pool", bufs=3))
+        g_pool = stack.enter_context(tc.tile_pool(name="g_pool", bufs=2))
+        t_pool = stack.enter_context(tc.tile_pool(name="t_pool", bufs=2))
         xg_pool = stack.enter_context(tc.tile_pool(name="xg_pool", bufs=3))
-        wq_pool = stack.enter_context(tc.tile_pool(name="wq_pool", bufs=3))
-        xq_pool = stack.enter_context(tc.tile_pool(name="xq_pool", bufs=4))
-        o_pool = stack.enter_context(tc.tile_pool(name="o_pool", bufs=4))
+        wq_pool = stack.enter_context(tc.tile_pool(name="wq_pool", bufs=4))
+        xq_pool = stack.enter_context(tc.tile_pool(name="xq_pool", bufs=6))
+        o_pool = stack.enter_context(tc.tile_pool(name="o_pool", bufs=6))
         psum_w = stack.enter_context(tc.psum_pool(name="psum_w", bufs=4))
         psum_x = stack.enter_context(tc.psum_pool(name="psum_x", bufs=2))
         psum_o = stack.enter_context(tc.psum_pool(name="psum_o", bufs=2))
 
         ident = const.tile([P, P], F32)
         make_identity(nc, ident[:])
-        ident_b = const.tile([P, P], BF16)
-        nc.vector.tensor_copy(out=ident_b[:], in_=ident[:])
 
         w_raw = {}
         x_raw = {}
-        x_pair = {}
         w_bank = {}
         x_bank = {}
         w_grp = {}
+        x_grp = {}
         w_codes = {}
         w_scales = {}
         x_codes = {}
         x_scales = {}
-        x_grp = {}
         acc = {}
         o_sb = {}
 
-        def load_w(q):
-            w_raw[q] = w_pool.tile([P, D_IN * D_OUT // 2], BF16, name="w_raw")
-            for u in range(2):
-                nc.sync.dma_start(
-                    out=w_raw[q][u:P:2, :].rearrange("p (g c) -> p g c", g=16), in_=w_view[q, u]
-                )
+        def load_w(s):
+            w_raw[s] = w_pool.tile([P, D_IN * D_OUT], BF16, name="w_raw")
+            nc.sync.dma_start(out=w_raw[s][:], in_=w_view[s])
 
-        def load_x(q0, nq):
-            t = x_pool.tile([P, 2 * GR * D_IN], BF16, name="x_raw")
-            width = nq * GR * D_IN
-            nc.sync.dma_start(out=t[:, 0:width], in_=x_view[:, q0 * GR * D_IN : q0 * GR * D_IN + width])
-            for k in range(nq):
-                x_raw[q0 + k] = t[:, k * GR * D_IN : (k + 1) * GR * D_IN]
-
-        def x_pairs(q):
-            x_pair[q] = p_pool.tile([P, GR * D_IN], BF16, name="x_pair")
-            nc.vector.tensor_copy(
-                out=x_pair[q][:].rearrange("b (e h j u) -> b e h j u", e=2, j=8, u=2),
-                in_=x_raw[q].rearrange("b (h u j e) -> b e h j u", u=2, j=8, e=2),
-            )
-
-        def w_transposes(q):
-            rows = w_raw[q][:].rearrange("r (a e o) -> r e o a", e=2, o=D_OUT)
-            for g in range(4):
-                wt = psum_w.tile([P, 1024], BF16, name="wt")
-                w_bank[(q, g)] = wt
-                dst = wt[:].rearrange("p (o e r) -> p o e r", o=4, e=2)
-                for o in range(4):
-                    for e in range(2):
-                        nc.tensor.transpose(dst[:, o, e], rows[:, e, 4 * g + o, :], ident_b[:])
-
-        def w_copy(q, g, engine):
-            if q not in w_grp:
-                w_grp[q] = g_pool.tile([P, GR * COLS * 4], BF16, name="w_grp", align_bytes=64)
-            dst = w_grp[q][:].bitcast(F32).rearrange("p (c g w) -> p c g w", g=4, w=8)[:, :, g, :]
-            src = w_bank[(q, g)][:].bitcast(F32).rearrange("p (w c) -> p c w", w=8)
-            if engine == "v":
-                nc.vector.tensor_copy(out=dst, in_=src)
-            else:
-                nc.scalar.copy(out=dst, in_=src)
-
-        def x_transposes(q):
-            words = x_pair[q][:].bitcast(F32).rearrange("b (e n a) -> b e n a", e=2, n=GR)
-            for h in range(2):
-                xt = psum_x.tile([P, 2, 2, P], F32, name="xt")
-                x_bank[(q, h)] = xt
-                for n in range(2):
-                    for e in range(2):
-                        nc.tensor.transpose(xt[:, n, e, :], words[:, e, 2 * h + n, :], ident[:])
-
-        def x_copy(q, h, engine):
-            if q not in x_grp:
-                x_grp[q] = xg_pool.tile([P, GR * D_IN], BF16, name="x_grp", align_bytes=64)
-            dst = x_grp[q][:].bitcast(F32).rearrange("p (h n b e) -> p h n b e", h=2, n=2, e=2)[:, h]
-            src = x_bank[(q, h)][:].rearrange("p n e b -> p n b e")
-            if engine == "v":
-                nc.vector.tensor_copy(out=dst, in_=src)
-            else:
-                nc.scalar.copy(out=dst, in_=src)
-
-        def x_quant(q):
-            x_codes[q] = xq_pool.tile([P, GR * P], U32, name="x_codes", align_bytes=64)
-            x_scales[q] = xq_pool.tile([P, GR * P], U8, name="x_scales", align_bytes=64)
-            nc.vector.quantize_mx(out=x_codes[q][:].bitcast(FP8X4), scales=x_scales[q][:], in_=x_grp[q][:])
-
-        def w_quant(q, parts):
-            w_codes[q] = wq_pool.tile([P, GR * COLS], U32, name="w_codes", align_bytes=64)
-            w_scales[q] = wq_pool.tile([P, GR * COLS], U8, name="w_scales", align_bytes=64)
-            width = GR * COLS // parts
+        def load_x(s, parts):
+            t = x_pool.tile([P, CH * D_IN], BF16, name="x_raw")
+            width = CH * D_IN // parts
             for k in range(parts):
-                cols = slice(k * width, (k + 1) * width)
+                lo = s * CH * D_IN + k * width
+                nc.sync.dma_start(out=t[:, k * width : (k + 1) * width], in_=x_view[:, lo : lo + width])
+            for b in range(2):
+                x_raw[2 * s + b] = t[:, b * HC * D_IN : (b + 1) * HC * D_IN]
+
+        def w_transposes(s, j):
+            words = w_raw[s][:].bitcast(F32).rearrange("r (a t j) -> r t j a", t=4, j=8)
+            wt = psum_w.tile([P, 512], F32, name="wt")
+            w_bank[(s, j)] = wt
+            for t in range(4):
+                nc.tensor.transpose(wt[:, t * P : (t + 1) * P], words[:, t, j, :], ident[:])
+
+        def w_copy(s, j, engine):
+            if s not in w_grp:
+                w_grp[s] = g_pool.tile([P, CH, 8, 32, 4], BF16, name="w_grp", align_bytes=64)
+            dst = w_grp[s][:, :, j, :, :]
+            src = w_bank[(s, j)][:].bitcast(BF16).rearrange("p (t n c) -> p n c t", t=4, n=CH)
+            if engine in "gh":
+                tmp = t_pool.tile([P, 512], F32, name="tmp")
+                if engine == "g":
+                    nc.vector.tensor_copy(out=tmp[:], in_=w_bank[(s, j)][:])
+                else:
+                    nc.scalar.copy(out=tmp[:], in_=w_bank[(s, j)][:])
+                nc.gpsimd.tensor_scalar(
+                    out=dst,
+                    in0=tmp[:].bitcast(BF16).rearrange("p (t n c) -> p n c t", t=4, n=CH),
+                    scalar1=1.0,
+                    scalar2=0.0,
+                    op0=MULT,
+                    op1=ADD,
+                )
+            elif engine == "v":
+                nc.vector.tensor_copy(out=dst, in_=src)
+            else:
+                nc.scalar.copy(out=dst, in_=src)
+
+        def w_quant(h, parts):
+            s, b = divmod(h, 2)
+            w_codes[h] = wq_pool.tile([P, HC * COLS], U32, name="w_codes", align_bytes=64)
+            w_scales[h] = wq_pool.tile([P, HC * COLS], U8, name="w_scales", align_bytes=64)
+            caps = HC // parts
+            for k in range(parts):
+                cols = slice(k * caps * COLS, (k + 1) * caps * COLS)
+                n0 = b * HC + k * caps
                 nc.vector.quantize_mx(
-                    out=w_codes[q][:, cols].bitcast(FP8X4),
-                    scales=w_scales[q][:, cols],
-                    in_=w_grp[q][:, 4 * k * width : 4 * (k + 1) * width],
+                    out=w_codes[h][:, cols].bitcast(FP8X4),
+                    scales=w_scales[h][:, cols],
+                    in_=w_grp[s][:, n0 : n0 + caps].rearrange("p n j c t -> p (n j c t)"),
                 )
 
-        def multiply(q, h):
+        def x_transposes(h):
+            words = x_raw[h].bitcast(F32).rearrange("b (n a v) -> b n v a", n=HC, v=2)
+            for g in range(2):
+                xt = psum_x.tile([P, 2, 2, P], F32, name="xt")
+                x_bank[(h, g)] = xt
+                for n in range(2):
+                    for v in range(2):
+                        nc.tensor.transpose(xt[:, n, v, :], words[:, 2 * g + n, v, :], ident[:])
+
+        def x_copy(h, g, engine):
+            if h not in x_grp:
+                x_grp[h] = xg_pool.tile([P, HC * D_IN], BF16, name="x_grp", align_bytes=64)
+            dst = x_grp[h][:].bitcast(F32).rearrange("p (g n b v) -> p g n b v", g=2, n=2, v=2)[:, g]
+            src = x_bank[(h, g)][:].rearrange("p n v b -> p n b v")
+            if engine == "v":
+                nc.vector.tensor_copy(out=dst, in_=src)
+            else:
+                nc.scalar.copy(out=dst, in_=src)
+
+        def x_quant(h):
+            x_codes[h] = xq_pool.tile([P, HC * P], U32, name="x_codes", align_bytes=64)
+            x_scales[h] = xq_pool.tile([P, HC * P], U8, name="x_scales", align_bytes=64)
+            nc.vector.quantize_mx(out=x_codes[h][:].bitcast(FP8X4), scales=x_scales[h][:], in_=x_grp[h][:])
+
+        def multiply(h, g):
             bank = psum_o.tile([P, 2, COLS], F32, name="acc")
-            acc[(q, h)] = bank
+            acc[(h, g)] = bank
             for n in range(2):
-                a = 2 * h + n
+                a = 2 * g + n
                 nc.tensor.matmul_mx(
                     out=bank[:, n, :],
-                    lhsT=x_codes[q][:, a * P : (a + 1) * P].bitcast(FP8X4),
-                    lhsT_scale=x_scales[q][:, a * P : (a + 1) * P],
-                    rhs=w_codes[q][:, a * COLS : (a + 1) * COLS].bitcast(FP8X4),
-                    rhs_scale=w_scales[q][:, a * COLS : (a + 1) * COLS],
+                    lhsT=x_codes[h][:, a * P : (a + 1) * P].bitcast(FP8X4),
+                    lhsT_scale=x_scales[h][:, a * P : (a + 1) * P],
+                    rhs=w_codes[h][:, a * COLS : (a + 1) * COLS].bitcast(FP8X4),
+                    rhs_scale=w_scales[h][:, a * COLS : (a + 1) * COLS],
                     start=True,
                     stop=True,
                 )
 
-        def evacuate(q, h, engine):
-            if q // 2 not in o_sb:
-                o_sb[q // 2] = o_pool.tile([P, 2 * GR, COLS], F32, name="o_sb")
-            n0 = GR * (q % 2) + 2 * h
-            dst = o_sb[q // 2][:, n0 : n0 + 2, :]
-            src = acc[(q, h)][:]
-            if engine == "v":
-                nc.vector.tensor_copy(out=dst, in_=src)
+        def evacuate(h, g, engine):
+            if h not in o_sb:
+                o_sb[h] = o_pool.tile([P, HC, COLS], F32, name="o_sb")
+            res = o_sb[h]
+            bank = acc[(h, g)]
+            if engine == "s":
+                for n in range(2):
+                    nc.scalar.copy(
+                        out=res[:, 2 * g + n, :].rearrange("p (m j e) -> p m j e", m=N_OUT, j=8),
+                        in_=bank[:, n, :].rearrange("p (j m e) -> p m j e", j=8, m=N_OUT),
+                    )
             else:
-                nc.scalar.copy(out=dst, in_=src)
+                nc.vector.tensor_copy(
+                    out=res[:, 2 * g : 2 * g + 2, :].rearrange("p n (m j e) -> p n m j e", m=N_OUT, j=8),
+                    in_=bank[:].rearrange("p n (j m e) -> p n m j e", j=8, m=N_OUT),
+                )
 
-        def store(n0, caps):
-            res = o_sb[n0 // (2 * GR)]
-            k0 = n0 % (2 * GR)
-            nc.sync.dma_start(
-                out=o_view[:, n0 * COLS : (n0 + caps) * COLS],
-                in_=res[:, k0 : k0 + caps, :].rearrange("p n c -> p (n c)"),
-            )
-
-        x_units = [(0, 1), (1, 1)] + [(q, 2) for q in range(2, N_Q, 2)]
-        first_loads = []
-        for k in range(W_BUFS):
-            first_loads.append(("w", k))
-            for j in range(X_BUFS):
-                if x_units[j][0] == k:
-                    first_loads.append(("x", j))
-
-        def refill_x(q):
-            for k in range(X_BUFS, len(x_units)):
-                freed = x_units[k - X_BUFS]
-                if freed[0] + freed[1] - 1 == q:
-                    load_x(x_units[k][0], x_units[k][1])
+        def store(h, parts):
+            caps = HC // parts
+            for k in range(parts):
+                lo = (h * HC + k * caps) * COLS
+                nc.sync.dma_start(
+                    out=o_view[:, lo : lo + caps * COLS],
+                    in_=o_sb[h][:, k * caps : (k + 1) * caps, :].rearrange("p n c -> p (n c)"),
+                )
 
         with tc.manual_schedule():
-            for kind, k in first_loads:
-                if kind == "w":
-                    load_w(k)
+            load_x(0, 4)
+            load_w(0)
+            for s in range(1, W_BUFS):
+                if s < X_BUFS:
+                    load_x(s, 1)
+                load_w(s)
+            for u in range(2):
+                x_transposes(u)
+                x_copy(u, 0, "s")
+                x_copy(u, 1, "v")
+            x_quant(0)
+            load_x(X_BUFS, 1)
+            for k in range(4 * N_CH):
+                s, q = divmod(k, 4)
+                w_transposes(s, 2 * q)
+                w_transposes(s, 2 * q + 1)
+                if q == 3 and s + W_BUFS < N_CH:
+                    load_w(s + W_BUFS)
+                w_copy(s, 2 * q, ROUTE[2 * q])
+                w_copy(s, 2 * q + 1, ROUTE[2 * q + 1])
+                if k % 2 == 0:
+                    u = k // 2 + 1
+                    if 2 <= u < N_H:
+                        x_copy(u, 0, "s")
+                        x_copy(u, 1, "s")
+                    u = k // 2 - 2
+                    if 0 <= u:
+                        w_quant(u, 1)
+                    u = k // 2 - 3
+                    if 0 <= u:
+                        multiply(u, 0)
+                        multiply(u, 1)
                 else:
-                    load_x(x_units[k][0], x_units[k][1])
-            x_pairs(0)
-            refill_x(0)
-            for s in range(-1, N_Q):
-                if s + 1 < N_Q:
-                    x_transposes(s + 1)
-                if s >= 2:
-                    for h in range(2):
-                        multiply(s - 2, h)
-                if s + 2 < N_Q:
-                    x_pairs(s + 2)
-                    refill_x(s + 2)
-                if s >= 0:
-                    for g in range(4):
-                        w_copy(s, g, "s")
-                if s + 1 < N_Q:
-                    x_copy(s + 1, 0, "s")
-                    x_copy(s + 1, 1, "v")
-                if s >= 2:
-                    evacuate(s - 2, 0, "s")
-                    evacuate(s - 2, 1, "v" if s % 2 else "s")
-                    if s % 2 == 1:
-                        store((s - 3) * GR, 2 * GR)
-                if s >= 1:
-                    w_quant(s - 1, 1)
-                if s >= 0:
-                    x_quant(s)
-                if s + 1 < N_Q:
-                    w_transposes(s + 1)
-                    if s + 1 + W_BUFS < N_Q:
-                        load_w(s + 1 + W_BUFS)
-            q = N_Q - 2
-            multiply(q, 0)
-            multiply(q, 1)
-            w_quant(q + 1, 2)
-            evacuate(q, 0, "s")
-            evacuate(q, 1, "s")
-            store(q * GR, GR)
-            q = N_Q - 1
-            multiply(q, 0)
-            multiply(q, 1)
-            evacuate(q, 0, "s")
-            store(q * GR, 2)
-            evacuate(q, 1, "v")
-            store(q * GR + 2, 2)
+                    u = (k - 7) // 2
+                    if 0 <= u:
+                        evacuate(u, 0, "s")
+                        evacuate(u, 1, "v" if q == 1 else "s")
+                        store(u, 1)
+                    u = (k + 3) // 2
+                    if u < N_H:
+                        x_transposes(u)
+                        if u % 2 == 1 and u // 2 + X_BUFS < N_CH:
+                            load_x(u // 2 + X_BUFS, 1)
+                    u = (k + 1) // 2
+                    if u < N_H:
+                        x_quant(u)
+            w_quant(N_H - 2, 2)
+            multiply(N_H - 3, 0)
+            multiply(N_H - 3, 1)
+            w_quant(N_H - 1, 2)
+            for u in range(N_H - 3, N_H):
+                if u > N_H - 3:
+                    multiply(u, 0)
+                    multiply(u, 1)
+                evacuate(u, 0, "s")
+                evacuate(u, 1, "s" if u < N_H - 1 else "v")
+                store(u, 1 if u < N_H - 1 else 2)

@@ -19,9 +19,11 @@ D_OUT = 16
 COLS = N_OUT * D_OUT
 CH = 8
 HC = 4
-N_CH = N_IN // CH
+N_CH = 7
 N_H = N_IN // HC
-W_BUFS = 5
+N_C = 2 * N_CH
+DIRECT = "gggg"
+W_BUFS = 4
 X_BUFS = 4
 ROUTE = "svsvsvsv"
 EVAC = "ssss"
@@ -32,6 +34,7 @@ FLOPS = 2 * P * N_IN * D_IN * COLS
 def tile_transforming_kernel(tc, inputs, transform_mat, out):
     nc = tc.nc
     w_view = transform_mat.rearrange("z (s n) m i o x -> s (z n m) (i o x)", n=CH)
+    d_view = transform_mat.rearrange("z (h n) m (p t) o x -> h p (z n m) (t o x)", n=HC, t=4)
     x_view = inputs.rearrange("b n i x -> b (n i x)")
     o_view = out.rearrange("b n m o x -> b (n m o x)")
 
@@ -40,6 +43,8 @@ def tile_transforming_kernel(tc, inputs, transform_mat, out):
         w_pool = stack.enter_context(tc.tile_pool(name="w_pool", bufs=W_BUFS))
         x_pool = stack.enter_context(tc.tile_pool(name="x_pool", bufs=X_BUFS))
         g_pool = stack.enter_context(tc.tile_pool(name="g_pool", bufs=2))
+        d_pool = stack.enter_context(tc.tile_pool(name="d_pool", bufs=2))
+        dg_pool = stack.enter_context(tc.tile_pool(name="dg_pool", bufs=2))
         t_pool = stack.enter_context(tc.tile_pool(name="t_pool", bufs=2))
         xg_pool = stack.enter_context(tc.tile_pool(name="xg_pool", bufs=3))
         wq_pool = stack.enter_context(tc.tile_pool(name="wq_pool", bufs=4))
@@ -53,6 +58,8 @@ def tile_transforming_kernel(tc, inputs, transform_mat, out):
         make_identity(nc, ident[:])
 
         w_raw = {}
+        d_raw = {}
+        d_grp = {}
         x_raw = {}
         w_bank = {}
         x_bank = {}
@@ -68,6 +75,25 @@ def tile_transforming_kernel(tc, inputs, transform_mat, out):
         def load_w(s):
             w_raw[s] = w_pool.tile([P, D_IN * D_OUT], BF16, name="w_raw")
             nc.sync.dma_start(out=w_raw[s][:], in_=w_view[s])
+
+        def load_d(u, parts):
+            d_raw[u] = d_pool.tile([P, HC * N_OUT, 4 * D_OUT], BF16, name="d_raw")
+            width = HC * N_OUT // parts
+            for k in range(parts):
+                rows = slice(k * width, (k + 1) * width)
+                nc.sync.dma_start(out=d_raw[u][:, rows, :], in_=d_view[u][:, rows, :])
+
+        def d_copy(u, n, engine):
+            if u not in d_grp:
+                d_grp[u] = dg_pool.tile([P, HC, N_OUT, D_OUT, 4], BF16, name="d_grp", align_bytes=64)
+            dst = d_grp[u][:, n]
+            src = d_raw[u][:, n * N_OUT : (n + 1) * N_OUT, :].rearrange("p m (t o) -> p m o t", t=4)
+            if engine == "v":
+                nc.vector.tensor_copy(out=dst, in_=src)
+            elif engine == "s":
+                nc.scalar.copy(out=dst, in_=src)
+            else:
+                nc.gpsimd.tensor_scalar(out=dst, in0=src, scalar1=1.0, scalar2=0.0, op0=MULT, op1=ADD)
 
         def load_x(s, parts):
             t = x_pool.tile([P, CH * D_IN], BF16, name="x_raw")
@@ -116,11 +142,13 @@ def tile_transforming_kernel(tc, inputs, transform_mat, out):
             caps = HC // parts
             for k in range(parts):
                 cols = slice(k * caps * COLS, (k + 1) * caps * COLS)
-                n0 = b * HC + k * caps
+                if h < N_C:
+                    n0 = b * HC + k * caps
+                    grp = w_grp[s][:, n0 : n0 + caps].rearrange("p n j c t -> p (n j c t)")
+                else:
+                    grp = d_grp[h][:, k * caps : (k + 1) * caps].rearrange("p n m o t -> p (n m o t)")
                 nc.vector.quantize_mx(
-                    out=w_codes[h][:, cols].bitcast(FP8X4),
-                    scales=w_scales[h][:, cols],
-                    in_=w_grp[s][:, n0 : n0 + caps].rearrange("p n j c t -> p (n j c t)"),
+                    out=w_codes[h][:, cols].bitcast(FP8X4), scales=w_scales[h][:, cols], in_=grp
                 )
 
         def x_transposes(h):
@@ -167,7 +195,13 @@ def tile_transforming_kernel(tc, inputs, transform_mat, out):
                 o_sb[h] = o_pool.tile([P, HC, COLS], F32, name="o_sb")
             res = o_sb[h]
             bank = acc[(h, g)]
-            if engine == "s":
+            if h >= N_C:
+                dst = res[:, 2 * g : 2 * g + 2, :]
+                if engine == "s":
+                    nc.scalar.copy(out=dst, in_=bank[:])
+                else:
+                    nc.vector.tensor_copy(out=dst, in_=bank[:])
+            elif engine == "s":
                 for n in range(2):
                     nc.scalar.copy(
                         out=res[:, 2 * g + n, :].rearrange("p (m j e) -> p m j e", m=N_OUT, j=8),
@@ -191,10 +225,10 @@ def tile_transforming_kernel(tc, inputs, transform_mat, out):
         with tc.manual_schedule():
             load_x(0, 4)
             load_w(0)
-            for s in range(1, W_BUFS):
-                if s < X_BUFS:
-                    load_x(s, 1)
-                load_w(s)
+            for s in range(1, X_BUFS):
+                load_x(s, 1)
+                if s < W_BUFS:
+                    load_w(s)
             for u in range(2):
                 x_transposes(u)
                 x_copy(u, 0, "s")
@@ -207,8 +241,15 @@ def tile_transforming_kernel(tc, inputs, transform_mat, out):
                 w_transposes(s, 2 * q + 1)
                 if q == 3 and s + W_BUFS < N_CH:
                     load_w(s + W_BUFS)
+                if q == 3 and s + W_BUFS == N_CH - 1:
+                    load_d(N_C, 4)
+                    load_d(N_C + 1, 4)
                 w_copy(s, 2 * q, ROUTE[2 * q])
                 w_copy(s, 2 * q + 1, ROUTE[2 * q + 1])
+                if k >= 4 * N_CH - 10:
+                    c = k - (4 * N_CH - 10)
+                    if c < 2 * HC:
+                        d_copy(N_C + c // HC, c % HC, DIRECT[c % HC])
                 if k % 2 == 0:
                     u = k // 2 + 1
                     if 2 <= u < N_H:
@@ -225,24 +266,37 @@ def tile_transforming_kernel(tc, inputs, transform_mat, out):
                     u = (k - 7) // 2
                     if 0 <= u:
                         evacuate(u, 0, "s")
-                        evacuate(u, 1, "v" if q == 1 else "s")
+                        evacuate(u, 1, "s")
                         store(u, 1)
                     u = (k + 3) // 2
                     if u < N_H:
                         x_transposes(u)
-                        if u % 2 == 1 and u // 2 + X_BUFS < N_CH:
+                        if u % 2 == 1 and u // 2 + X_BUFS < N_H // 2:
                             load_x(u // 2 + X_BUFS, 1)
                     u = (k + 1) // 2
                     if u < N_H:
                         x_quant(u)
-            w_quant(N_H - 2, 2)
-            multiply(N_H - 3, 0)
-            multiply(N_H - 3, 1)
-            w_quant(N_H - 1, 2)
-            for u in range(N_H - 3, N_H):
-                if u > N_H - 3:
-                    multiply(u, 0)
-                    multiply(u, 1)
+                    if k == 4 * N_CH - 3:
+                        w_quant(N_C, 1)
+            x_copy(N_H - 1, 0, "s")
+            x_copy(N_H - 1, 1, "s")
+            w_quant(N_C - 2, 1)
+            multiply(N_C - 3, 0)
+            multiply(N_C - 3, 1)
+            evacuate(N_C - 3, 0, "s")
+            evacuate(N_C - 3, 1, "s")
+            store(N_C - 3, 1)
+            multiply(N_C, 0)
+            multiply(N_C, 1)
+            w_quant(N_C - 1, 1)
+            evacuate(N_C, 0, "s")
+            evacuate(N_C, 1, "s")
+            store(N_C, 1)
+            x_quant(N_C + 1)
+            w_quant(N_C + 1, 1)
+            for u in (N_C - 2, N_C - 1, N_C + 1):
+                multiply(u, 0)
+                multiply(u, 1)
                 evacuate(u, 0, "s")
-                evacuate(u, 1, "s" if u < N_H - 1 else "v")
-                store(u, 1 if u < N_H - 1 else 2)
+                evacuate(u, 1, "v")
+                store(u, 1 if u <= N_C else 2)

@@ -114,8 +114,8 @@ def tile_transforming_kernel(tc, inputs, transform_mat, out):
         def w_copy(s, j, engine):
             if s not in w_grp:
                 w_grp[s] = g_pool.tile([P, CH, 8, 32, 4], BF16, name="w_grp", align_bytes=64)
-            dst = w_grp[s][:, :, j, :, :]
-            src = w_bank[(s, j)][:].bitcast(BF16).rearrange("p (t n c) -> p n c t", t=4, n=CH)
+            dst = w_grp[s][:, :, j, :, :].rearrange("p n (c i) t -> p n c t i", i=4)
+            src = w_bank[(s, j)][:].bitcast(BF16).rearrange("p (t n c i) -> p n c t i", t=4, n=CH, i=4)
             if engine in "gh":
                 tmp = t_pool.tile([P, 512], F32, name="tmp")
                 if engine == "g":
@@ -201,17 +201,13 @@ def tile_transforming_kernel(tc, inputs, transform_mat, out):
                     nc.scalar.copy(out=dst, in_=bank[:])
                 else:
                     nc.vector.tensor_copy(out=dst, in_=bank[:])
-            elif engine == "s":
-                for n in range(2):
-                    nc.scalar.copy(
-                        out=res[:, 2 * g + n, :].rearrange("p (m j e) -> p m j e", m=N_OUT, j=8),
-                        in_=bank[:, n, :].rearrange("p (j m e) -> p m j e", j=8, m=N_OUT),
-                    )
             else:
-                nc.vector.tensor_copy(
-                    out=res[:, 2 * g : 2 * g + 2, :].rearrange("p n (m j e) -> p n m j e", m=N_OUT, j=8),
-                    in_=bank[:].rearrange("p n (j m e) -> p n m j e", j=8, m=N_OUT),
-                )
+                dst = res[:, 2 * g : 2 * g + 2, :].rearrange("p n (m j e) -> p n m j e", m=N_OUT, j=8)
+                src = bank[:].rearrange("p n (j m e) -> p n m j e", j=8, m=N_OUT)
+                if engine == "s":
+                    nc.scalar.copy(out=dst, in_=src)
+                else:
+                    nc.vector.tensor_copy(out=dst, in_=src)
 
         def store(h, parts):
             caps = HC // parts

@@ -113,9 +113,9 @@ def tile_transforming_kernel(tc, inputs, transform_mat, out):
 
         def w_copy(s, j, engine):
             if s not in w_grp:
-                w_grp[s] = g_pool.tile([P, CH, 8, 32, 4], BF16, name="w_grp", align_bytes=64)
-            dst = w_grp[s][:, :, j, :, :].rearrange("p n (c i) t -> p n c t i", i=4)
-            src = w_bank[(s, j)][:].bitcast(BF16).rearrange("p (t n c i) -> p n c t i", t=4, n=CH, i=4)
+                w_grp[s] = g_pool.tile([P, CH, COLS, 4], BF16, name="w_grp", align_bytes=64)
+            dst = w_grp[s][:].rearrange("p n (m r j w) t -> p j (n m) t r w", r=2, j=8, w=2)[:, j]
+            src = w_bank[(s, j)][:].bitcast(BF16).rearrange("p (t m r w) -> p m t r w", t=4, r=2, w=2)
             if engine in "gh":
                 tmp = t_pool.tile([P, 512], F32, name="tmp")
                 if engine == "g":
@@ -144,7 +144,7 @@ def tile_transforming_kernel(tc, inputs, transform_mat, out):
                 cols = slice(k * caps * COLS, (k + 1) * caps * COLS)
                 if h < N_C:
                     n0 = b * HC + k * caps
-                    grp = w_grp[s][:, n0 : n0 + caps].rearrange("p n j c t -> p (n j c t)")
+                    grp = w_grp[s][:, n0 : n0 + caps].rearrange("p n c t -> p (n c t)")
                 else:
                     grp = d_grp[h][:, k * caps : (k + 1) * caps].rearrange("p n m o t -> p (n m o t)")
                 nc.vector.quantize_mx(
@@ -195,19 +195,11 @@ def tile_transforming_kernel(tc, inputs, transform_mat, out):
                 o_sb[h] = o_pool.tile([P, HC, COLS], F32, name="o_sb")
             res = o_sb[h]
             bank = acc[(h, g)]
-            if h >= N_C:
-                dst = res[:, 2 * g : 2 * g + 2, :]
-                if engine == "s":
-                    nc.scalar.copy(out=dst, in_=bank[:])
-                else:
-                    nc.vector.tensor_copy(out=dst, in_=bank[:])
+            dst = res[:, 2 * g : 2 * g + 2, :]
+            if engine == "s":
+                nc.scalar.copy(out=dst, in_=bank[:])
             else:
-                dst = res[:, 2 * g : 2 * g + 2, :].rearrange("p n (m j e) -> p n m j e", m=N_OUT, j=8)
-                src = bank[:].rearrange("p n (j m e) -> p n m j e", j=8, m=N_OUT)
-                if engine == "s":
-                    nc.scalar.copy(out=dst, in_=src)
-                else:
-                    nc.vector.tensor_copy(out=dst, in_=src)
+                nc.vector.tensor_copy(out=dst, in_=bank[:])
 
         def store(h, parts):
             caps = HC // parts

@@ -76,12 +76,11 @@ def tile_transforming_kernel(tc, inputs, transform_mat, out):
             w_raw[s] = w_pool.tile([P, D_IN * D_OUT], BF16, name="w_raw")
             nc.sync.dma_start(out=w_raw[s][:], in_=w_view[s])
 
-        def load_d(u, parts):
-            d_raw[u] = d_pool.tile([P, HC * N_OUT, 4 * D_OUT], BF16, name="d_raw")
-            width = HC * N_OUT // parts
-            for k in range(parts):
-                rows = slice(k * width, (k + 1) * width)
-                nc.sync.dma_start(out=d_raw[u][:, rows, :], in_=d_view[u][:, rows, :])
+        def load_d(u, n):
+            if n == 0:
+                d_raw[u] = d_pool.tile([P, HC * N_OUT, 4 * D_OUT], BF16, name="d_raw")
+            rows = slice(n * N_OUT, (n + 1) * N_OUT)
+            nc.sync.dma_start(out=d_raw[u][:, rows, :], in_=d_view[u][:, rows, :])
 
         def d_copy(u, n, engine):
             if u not in d_grp:
@@ -114,23 +113,9 @@ def tile_transforming_kernel(tc, inputs, transform_mat, out):
         def w_copy(s, j, engine):
             if s not in w_grp:
                 w_grp[s] = g_pool.tile([P, CH, COLS, 4], BF16, name="w_grp", align_bytes=64)
-            dst = w_grp[s][:].rearrange("p n (m r j w) t -> p j (n m) t r w", r=2, j=8, w=2)[:, j]
-            src = w_bank[(s, j)][:].bitcast(BF16).rearrange("p (t m r w) -> p m t r w", t=4, r=2, w=2)
-            if engine in "gh":
-                tmp = t_pool.tile([P, 512], F32, name="tmp")
-                if engine == "g":
-                    nc.vector.tensor_copy(out=tmp[:], in_=w_bank[(s, j)][:])
-                else:
-                    nc.scalar.copy(out=tmp[:], in_=w_bank[(s, j)][:])
-                nc.gpsimd.tensor_scalar(
-                    out=dst,
-                    in0=tmp[:].bitcast(BF16).rearrange("p (t n c) -> p n c t", t=4, n=CH),
-                    scalar1=1.0,
-                    scalar2=0.0,
-                    op0=MULT,
-                    op1=ADD,
-                )
-            elif engine == "v":
+            dst = w_grp[s][:].rearrange("p n (m j w) t -> p j (n m) w t", j=8, w=2)[:, j]
+            src = w_bank[(s, j)][:].bitcast(BF16).rearrange("p (t r w) -> p r w t", t=4, w=2)
+            if engine == "v":
                 nc.vector.tensor_copy(out=dst, in_=src)
             else:
                 nc.scalar.copy(out=dst, in_=src)
@@ -229,13 +214,13 @@ def tile_transforming_kernel(tc, inputs, transform_mat, out):
                 w_transposes(s, 2 * q + 1)
                 if q == 3 and s + W_BUFS < N_CH:
                     load_w(s + W_BUFS)
-                if q == 3 and s + W_BUFS == N_CH - 1:
-                    load_d(N_C, 4)
-                    load_d(N_C + 1, 4)
+                c, step = divmod(k - 7, 2)
+                if 0 <= c < 2 * HC and step == 0:
+                    load_d(N_C + c // HC, c % HC)
                 w_copy(s, 2 * q, ROUTE[2 * q])
                 w_copy(s, 2 * q + 1, ROUTE[2 * q + 1])
-                if k >= 4 * N_CH - 10:
-                    c = k - (4 * N_CH - 10)
+                c = k - (4 * N_CH - 10)
+                if 0 <= c:
                     if c < 2 * HC:
                         d_copy(N_C + c // HC, c % HC, DIRECT[c % HC])
                 if k % 2 == 0:

from contextlib import ExitStack

import concourse.mybir as mybir
from concourse.masks import make_identity

F32 = mybir.dt.float32
BF16 = mybir.dt.bfloat16
MULT = mybir.AluOpType.mult
ADD = mybir.AluOpType.add
U32 = mybir.dt.uint32
U8 = mybir.dt.uint8
FP8X4 = mybir.dt.float8_e4m3fn_x4

P = 128
N_IN = 64
N_OUT = 16
D_IN = 512
D_OUT = 16
COLS = N_OUT * D_OUT
CH = 8
HC = 4
N_CH = 7
N_H = N_IN // HC
N_C = 2 * N_CH
DIRECT = "gggg"
W_BUFS = 4
X_BUFS = 4
ROUTE = "svsvsvsv"
EVAC = "ssss"

FLOPS = 2 * P * N_IN * D_IN * COLS


def tile_transforming_kernel(tc, inputs, transform_mat, out):
    nc = tc.nc
    w_view = transform_mat.rearrange("z (s n) m i o x -> s (z n m) (i o x)", n=CH)
    d_view = transform_mat.rearrange("z (h n) m (p t) o x -> h p (z n m) (t o x)", n=HC, t=4)
    x_view = inputs.rearrange("b n i x -> b (n i x)")
    o_view = out.rearrange("b n m o x -> b (n m o x)")

    with ExitStack() as stack:
        const = stack.enter_context(tc.tile_pool(name="const", bufs=1))
        w_pool = stack.enter_context(tc.tile_pool(name="w_pool", bufs=W_BUFS))
        x_pool = stack.enter_context(tc.tile_pool(name="x_pool", bufs=X_BUFS))
        g_pool = stack.enter_context(tc.tile_pool(name="g_pool", bufs=2))
        d_pool = stack.enter_context(tc.tile_pool(name="d_pool", bufs=2))
        dg_pool = stack.enter_context(tc.tile_pool(name="dg_pool", bufs=2))
        t_pool = stack.enter_context(tc.tile_pool(name="t_pool", bufs=2))
        xg_pool = stack.enter_context(tc.tile_pool(name="xg_pool", bufs=3))
        wq_pool = stack.enter_context(tc.tile_pool(name="wq_pool", bufs=4))
        xq_pool = stack.enter_context(tc.tile_pool(name="xq_pool", bufs=6))
        o_pool = stack.enter_context(tc.tile_pool(name="o_pool", bufs=6))
        psum_w = stack.enter_context(tc.psum_pool(name="psum_w", bufs=4))
        psum_x = stack.enter_context(tc.psum_pool(name="psum_x", bufs=2))
        psum_o = stack.enter_context(tc.psum_pool(name="psum_o", bufs=2))

        ident = const.tile([P, P], F32)
        make_identity(nc, ident[:])

        w_raw = {}
        d_raw = {}
        d_grp = {}
        x_raw = {}
        w_bank = {}
        x_bank = {}
        w_grp = {}
        x_grp = {}
        w_codes = {}
        w_scales = {}
        x_codes = {}
        x_scales = {}
        acc = {}
        o_sb = {}

        def load_w(s):
            w_raw[s] = w_pool.tile([P, D_IN * D_OUT], BF16, name="w_raw")
            nc.sync.dma_start(out=w_raw[s][:], in_=w_view[s])

        def load_d(u, n):
            if n == 0:
                d_raw[u] = d_pool.tile([P, HC * N_OUT, 4 * D_OUT], BF16, name="d_raw")
            rows = slice(n * N_OUT, (n + 1) * N_OUT)
            nc.sync.dma_start(out=d_raw[u][:, rows, :], in_=d_view[u][:, rows, :])

        def d_copy(u, n, engine):
            if u not in d_grp:
                d_grp[u] = dg_pool.tile([P, HC, N_OUT, D_OUT, 4], BF16, name="d_grp", align_bytes=64)
            dst = d_grp[u][:, n]
            src = d_raw[u][:, n * N_OUT : (n + 1) * N_OUT, :].rearrange("p m (t o) -> p m o t", t=4)
            if engine == "v":
                nc.vector.tensor_copy(out=dst, in_=src)
            elif engine == "s":
                nc.scalar.copy(out=dst, in_=src)
            else:
                nc.gpsimd.tensor_scalar(out=dst, in0=src, scalar1=1.0, scalar2=0.0, op0=MULT, op1=ADD)

        def load_x(s, parts):
            t = x_pool.tile([P, CH * D_IN], BF16, name="x_raw")
            width = CH * D_IN // parts
            for k in range(parts):
                lo = s * CH * D_IN + k * width
                nc.sync.dma_start(out=t[:, k * width : (k + 1) * width], in_=x_view[:, lo : lo + width])
            for b in range(2):
                x_raw[2 * s + b] = t[:, b * HC * D_IN : (b + 1) * HC * D_IN]

        def w_transposes(s, j):
            words = w_raw[s][:].bitcast(F32).rearrange("r (a t j) -> r t j a", t=4, j=8)
            wt = psum_w.tile([P, 512], F32, name="wt")
            w_bank[(s, j)] = wt
            for t in range(4):
                nc.tensor.transpose(wt[:, t * P : (t + 1) * P], words[:, t, j, :], ident[:])

        def w_copy(s, j, engine):
            if s not in w_grp:
                w_grp[s] = g_pool.tile([P, CH, COLS, 4], BF16, name="w_grp", align_bytes=64)
            dst = w_grp[s][:].rearrange("p n (m j w) t -> p j (n m) w t", j=8, w=2)[:, j]
            src = w_bank[(s, j)][:].bitcast(BF16).rearrange("p (t r w) -> p r w t", t=4, w=2)
            if engine == "v":
                nc.vector.tensor_copy(out=dst, in_=src)
            else:
                nc.scalar.copy(out=dst, in_=src)

        def w_quant(h, parts):
            s, b = divmod(h, 2)
            w_codes[h] = wq_pool.tile([P, HC * COLS], U32, name="w_codes", align_bytes=64)
            w_scales[h] = wq_pool.tile([P, HC * COLS], U8, name="w_scales", align_bytes=64)
            caps = HC // parts
            for k in range(parts):
                cols = slice(k * caps * COLS, (k + 1) * caps * COLS)
                if h < N_C:
                    n0 = b * HC + k * caps
                    grp = w_grp[s][:, n0 : n0 + caps].rearrange("p n c t -> p (n c t)")
                else:
                    grp = d_grp[h][:, k * caps : (k + 1) * caps].rearrange("p n m o t -> p (n m o t)")
                nc.vector.quantize_mx(
                    out=w_codes[h][:, cols].bitcast(FP8X4), scales=w_scales[h][:, cols], in_=grp
                )

        def x_transposes(h):
            words = x_raw[h].bitcast(F32).rearrange("b (n a v) -> b n v a", n=HC, v=2)
            for g in range(2):
                xt = psum_x.tile([P, 2, 2, P], F32, name="xt")
                x_bank[(h, g)] = xt
                for n in range(2):
                    for v in range(2):
                        nc.tensor.transpose(xt[:, n, v, :], words[:, 2 * g + n, v, :], ident[:])

        def x_copy(h, g, engine):
            if h not in x_grp:
                x_grp[h] = xg_pool.tile([P, HC * D_IN], BF16, name="x_grp", align_bytes=64)
            dst = x_grp[h][:].bitcast(F32).rearrange("p (g n b v) -> p g n b v", g=2, n=2, v=2)[:, g]
            src = x_bank[(h, g)][:].rearrange("p n v b -> p n b v")
            if engine == "v":
                nc.vector.tensor_copy(out=dst, in_=src)
            else:
                nc.scalar.copy(out=dst, in_=src)

        def x_quant(h):
            x_codes[h] = xq_pool.tile([P, HC * P], U32, name="x_codes", align_bytes=64)
            x_scales[h] = xq_pool.tile([P, HC * P], U8, name="x_scales", align_bytes=64)
            nc.vector.quantize_mx(out=x_codes[h][:].bitcast(FP8X4), scales=x_scales[h][:], in_=x_grp[h][:])

        def multiply(h, g):
            bank = psum_o.tile([P, 2, COLS], F32, name="acc")
            acc[(h, g)] = bank
            for n in range(2):
                a = 2 * g + n
                nc.tensor.matmul_mx(
                    out=bank[:, n, :],
                    lhsT=x_codes[h][:, a * P : (a + 1) * P].bitcast(FP8X4),
                    lhsT_scale=x_scales[h][:, a * P : (a + 1) * P],
                    rhs=w_codes[h][:, a * COLS : (a + 1) * COLS].bitcast(FP8X4),
                    rhs_scale=w_scales[h][:, a * COLS : (a + 1) * COLS],
                    start=True,
                    stop=True,
                )

        def evacuate(h, g, engine):
            if h not in o_sb:
                o_sb[h] = o_pool.tile([P, HC, COLS], F32, name="o_sb")
            res = o_sb[h]
            bank = acc[(h, g)]
            dst = res[:, 2 * g : 2 * g + 2, :]
            if engine == "s":
                nc.scalar.copy(out=dst, in_=bank[:])
            else:
                nc.vector.tensor_copy(out=dst, in_=bank[:])

        def store(h, parts):
            caps = HC // parts
            for k in range(parts):
                lo = (h * HC + k * caps) * COLS
                nc.sync.dma_start(
                    out=o_view[:, lo : lo + caps * COLS],
                    in_=o_sb[h][:, k * caps : (k + 1) * caps, :].rearrange("p n c -> p (n c)"),
                )

        with tc.manual_schedule():
            load_x(0, 4)
            load_w(0)
            for s in range(1, X_BUFS):
                load_x(s, 1)
                if s < W_BUFS:
                    load_w(s)
            for u in range(2):
                x_transposes(u)
                x_copy(u, 0, "s")
                x_copy(u, 1, "v")
            x_quant(0)
            load_x(X_BUFS, 1)
            for k in range(4 * N_CH):
                s, q = divmod(k, 4)
                w_transposes(s, 2 * q)
                w_transposes(s, 2 * q + 1)
                if q == 3 and s + W_BUFS < N_CH:
                    load_w(s + W_BUFS)
                c, step = divmod(k - 7, 2)
                if 0 <= c < 2 * HC and step == 0:
                    load_d(N_C + c // HC, c % HC)
                w_copy(s, 2 * q, ROUTE[2 * q])
                w_copy(s, 2 * q + 1, ROUTE[2 * q + 1])
                c = k - (4 * N_CH - 10)
                if 0 <= c:
                    if c < 2 * HC:
                        d_copy(N_C + c // HC, c % HC, DIRECT[c % HC])
                if k % 2 == 0:
                    u = k // 2 + 1
                    if 2 <= u < N_H:
                        x_copy(u, 0, "s")
                        x_copy(u, 1, "s")
                    u = k // 2 - 2
                    if 0 <= u:
                        w_quant(u, 1)
                    u = k // 2 - 3
                    if 0 <= u:
                        multiply(u, 0)
                        multiply(u, 1)
                else:
                    u = (k - 7) // 2
                    if 0 <= u:
                        evacuate(u, 0, "s")
                        evacuate(u, 1, "s")
                        store(u, 1)
                    u = (k + 3) // 2
                    if u < N_H:
                        x_transposes(u)
                        if u % 2 == 1 and u // 2 + X_BUFS < N_H // 2:
                            load_x(u // 2 + X_BUFS, 1)
                    u = (k + 1) // 2
                    if u < N_H:
                        x_quant(u)
                    if k == 4 * N_CH - 3:
                        w_quant(N_C, 1)
            x_copy(N_H - 1, 0, "s")
            x_copy(N_H - 1, 1, "s")
            w_quant(N_C - 2, 1)
            multiply(N_C - 3, 0)
            multiply(N_C - 3, 1)
            evacuate(N_C - 3, 0, "s")
            evacuate(N_C - 3, 1, "s")
            store(N_C - 3, 1)
            multiply(N_C, 0)
            multiply(N_C, 1)
            w_quant(N_C - 1, 1)
            evacuate(N_C, 0, "s")
            evacuate(N_C, 1, "s")
            store(N_C, 1)
            x_quant(N_C + 1)
            w_quant(N_C + 1, 1)
            for u in (N_C - 2, N_C - 1, N_C + 1):
                multiply(u, 0)
                multiply(u, 1)
                evacuate(u, 0, "s")
                evacuate(u, 1, "v")
                store(u, 1 if u <= N_C else 2)
